import numpy as np
import ml_dtypes


def mxq(x, axis, fmt="e4m3"):
    dtype, down = {"e4m3": (ml_dtypes.float8_e4m3fn, 7), "e5m2": (ml_dtypes.float8_e5m2, 14)}[fmt]
    v = np.moveaxis(np.asarray(x, np.float32).astype(ml_dtypes.bfloat16).astype(np.float64), axis, -1)
    blocks = v.reshape(v.shape[:-1] + (-1, 32))
    amax = np.abs(blocks).max(-1, keepdims=True)
    byte = np.maximum(np.where(amax > 0, np.frexp(amax)[1] - 1 + 127, 0) - down, 1)
    scale = np.exp2(byte - 127.0)
    codes = (blocks / scale).astype(np.float32).astype(dtype).astype(np.float64)
    return np.moveaxis((codes * scale).reshape(v.shape), -1, axis)


WIDE = False


def mx_kscale(k):
    if not WIDE:
        return np.ones(k)
    levels = np.array([10, -10, 5, -5, 0])
    a = np.random.permutation(np.resize(levels, k // 512 * 4)).reshape(k // 512, 4)
    idx = np.arange(k)
    return np.exp2(a[idx // 512, idx % 128 // 32])


BF16 = ml_dtypes.bfloat16


def bf(x):
    return np.asarray(x, np.float32).astype(BF16)


def f64(x):
    return np.asarray(x).astype(np.float64)


B, T, C_IN, HIDDEN, HEADS, OUT_DIM = 4, 2048, 512, 512, 8, 512
RMS_EPS = 1.1920928955078125e-07


def silu(z):
    return z / (1.0 + np.exp(-z))


def setup_inputs():
    s, t = mx_kscale(C_IN), mx_kscale(HIDDEN)
    r = np.exp2(-12.0 * np.random.random((B, T, 1)))
    return {"x": bf(np.random.standard_normal((B, T, C_IN)) * s),
            "h_attn": bf(np.random.standard_normal((B, T, HIDDEN)) * 0.8 * r),
            "Wu": bf(np.random.standard_normal((HIDDEN, C_IN)) / np.sqrt(C_IN) / s),
            "bu": bf(np.random.standard_normal(HIDDEN) * 0.1),
            "g_norm": bf((1.0 + 0.1 * np.random.standard_normal(HIDDEN)) * t),
            "Wf": bf(np.random.standard_normal((OUT_DIM, HIDDEN)) / np.sqrt(HIDDEN) / t),
            "b_out": bf(np.random.standard_normal(OUT_DIM) * 0.1)}


def reference(x, h_attn, Wu, bu, g_norm, Wf, b_out):
    u = silu((mxq(f64(x), 2, "e4m3") @ mxq(f64(Wu), 1, "e4m3").T) + f64(bu))
    av = f64(h_attn)
    av_norm = av * (1.0 / np.sqrt(np.mean(av * av, axis=-1, keepdims=True) + RMS_EPS)) * f64(g_norm)
    uv = av_norm * u
    return (mxq(uv, 2, "e4m3") @ mxq(f64(Wf), 1, "e4m3").T) + f64(b_out)

@@ -1,0 +1,273 @@
+from contextlib import ExitStack
+
+import concourse.mybir as mybir
+from concourse.masks import make_identity
+
+FP8X4 = mybir.dt.float8_e4m3fn_x4
+BF16 = mybir.dt.bfloat16
+F32 = mybir.dt.float32
+U32 = mybir.dt.uint32
+U8 = mybir.dt.uint8
+ACT = mybir.ActivationFunctionType
+ALU = mybir.AluOpType
+
+P = 128
+PACK = 4
+WIDTH = P * PACK
+TOKENS = 4 * 2048
+TILES = 4
+GROUP = TILES * P
+N_GROUPS = TOKENS // GROUP
+N_TILES = TOKENS // P
+RMS_EPS = 1.1920928955078125e-07
+FLOPS = 2 * 2 * TOKENS * WIDTH * WIDTH
+
+
+def tile_hstu_pb_t_kernel(tc, x, h_attn, Wu, bu, g_norm, Wf, b_out, out):
+    nc = tc.nc
+    x_groups = x.flatten_outer_dims().rearrange("(n p j) c -> n p (j c)", p=P, j=TILES)
+    h_groups = h_attn.flatten_outer_dims().rearrange("(n p j) c -> n p (j c)", p=P, j=TILES)
+    out_groups = out.flatten_outer_dims().rearrange("(n p j) c -> n p (j c)", p=P, j=TILES)
+
+    with ExitStack() as ctx:
+        const = ctx.enter_context(tc.tile_pool(name="const", bufs=1))
+        loads = ctx.enter_context(tc.tile_pool(name="loads", bufs=4))
+        work = ctx.enter_context(tc.tile_pool(name="work", bufs=3))
+        psum = ctx.enter_context(tc.psum_pool(name="psum", bufs=2))
+
+        x_sb, h_sb, hn_sb, sumsq, rstd = {}, {}, {}, {}, {}
+        x_grouped, x_codes, x_scales = {}, {}, {}
+        u_sb, uv_grouped, uv_codes, uv_scales, o_sb = {}, {}, {}, {}, {}
+        xt_ps, z_ps, ht_ps, o_ps = {}, {}, {}, {}
+
+        def transpose_word_pair(rows, first):
+            words = rows[:].bitcast(F32)
+            bank = psum.tile([P, 2, 2, P], F32, name="xt", tag="xt")
+            for l in range(2):
+                for u in range(2):
+                    col = (first + l) * (WIDTH // 2) + u * P
+                    nc.tensor.transpose(bank[:, l, u, :], words[:, col : col + P], ident[:])
+            return bank
+
+        def regroup_word_pair(copy, bank, grouped, first):
+            words = grouped[:].bitcast(F32)[:, first * 2 * P : (first + 2) * 2 * P]
+            copy(
+                out=words.rearrange("p (l w u) -> p l w u", l=2, u=2),
+                in_=bank[:].rearrange("p l u w -> p l w u"),
+            )
+
+        def transpose_f32_tile(rows, first_col):
+            bank = psum.tile([P, PACK, P], F32, name="ht", tag="ht")
+            for t in range(PACK):
+                col = first_col + t * P
+                nc.tensor.transpose(bank[:, t, :], rows[:, col : col + P], ident[:])
+            return bank
+
+        def load(n):
+            x_sb[n] = loads.tile([P, TILES * WIDTH], BF16, name="x_sb", tag="x_sb")
+            nc.sync.dma_start(out=x_sb[n][:], in_=x_groups[n])
+            h_sb[n] = loads.tile([P, TILES * WIDTH], BF16, name="h_sb", tag="h_sb")
+            nc.sync.dma_start(out=h_sb[n][:], in_=h_groups[n])
+
+        def square_sum(n, j):
+            if j == 0:
+                sumsq[n] = work.tile([P, TILES], F32, name="sumsq", tag="sumsq")
+            squares = work.tile([P, WIDTH], BF16, name="squares", tag="squares")
+            nc.scalar.activation(
+                out=squares[:],
+                in_=h_sb[n][:, j * WIDTH : (j + 1) * WIDTH],
+                func=ACT.Square,
+                accum_out=sumsq[n][:, j : j + 1],
+            )
+
+        def inverse_rms(n):
+            mean = work.tile([P, TILES], F32, name="mean", tag="mean")
+            nc.gpsimd.tensor_scalar(
+                out=mean[:], in0=sumsq[n][:], scalar1=1.0 / WIDTH, scalar2=RMS_EPS, op0=ALU.mult, op1=ALU.add
+            )
+            rstd[n] = work.tile([P, TILES], F32, name="rstd", tag="rstd")
+            nc.gpsimd.tensor_tensor(out=rstd[n][:], in0=mean[:], in1=minus_half[:], op=ALU.pow)
+
+        def normalise(n, j):
+            if j == 0:
+                hn_sb[n] = work.tile([P, TILES * WIDTH], F32, name="hn_sb", tag="hn_sb")
+            cols = slice(j * WIDTH, (j + 1) * WIDTH)
+            nc.gpsimd.tensor_scalar(
+                out=hn_sb[n][:, cols],
+                in0=h_sb[n][:, cols],
+                scalar1=rstd[n][:, j : j + 1],
+                scalar2=0.0,
+                op0=ALU.mult,
+                op1=ALU.add,
+            )
+
+        def transpose_x(n, first):
+            xt_ps[n, first] = transpose_word_pair(x_sb[n], first)
+
+        def regroup_x(n, first):
+            if first == 0:
+                x_grouped[n] = work.tile([P, GROUP * PACK], BF16, name="x_grouped", tag="x_grouped", align_bytes=64)
+            regroup_word_pair(nc.scalar.copy, xt_ps[n, first], x_grouped[n], first)
+
+        def quantise_x(n):
+            x_codes[n] = work.tile([P, GROUP], U32, name="x_codes", tag="x_codes", align_bytes=64)
+            x_scales[n] = work.tile([P, GROUP], U8, name="x_scales", tag="x_scales", align_bytes=64)
+            nc.vector.quantize_mx(out=x_codes[n][:].bitcast(FP8X4), scales=x_scales[n][:], in_=x_grouped[n][:])
+
+        def project_up(n, t):
+            z_ps[n, t] = psum.tile([P, GROUP], F32, name="z", tag="z")
+            cols = slice(t * P, (t + 1) * P)
+            nc.tensor.matmul_mx(
+                out=z_ps[n, t][:],
+                lhsT=wu_codes[:, cols].bitcast(FP8X4),
+                lhsT_scale=wu_scales[:, cols],
+                rhs=x_codes[n][:].bitcast(FP8X4),
+                rhs_scale=x_scales[n][:],
+                start=True,
+                stop=True,
+            )
+
+        def silu(n, t):
+            if t == 0:
+                u_sb[n] = work.tile([P, PACK, GROUP], F32, name="u_sb", tag="u_sb")
+            nc.scalar.activation(
+                out=u_sb[n][:, t, :], in_=z_ps[n, t][:], func=ACT.Silu, bias=bias_gain[:, t : t + 1], scale=1.0
+            )
+
+        def gain(n, t):
+            nc.vector.tensor_scalar_mul(
+                out=u_sb[n][:, t, :], in0=u_sb[n][:, t, :], scalar1=bias_gain[:, PACK + t : PACK + t + 1]
+            )
+
+        def transpose_h(n, j):
+            ht_ps[n, j] = transpose_f32_tile(hn_sb[n], j * WIDTH)
+
+        def multiply(n, j):
+            if j == 0:
+                uv_grouped[n] = work.tile([P, GROUP, PACK], BF16, name="uv_grouped", tag="uv_grouped", align_bytes=64)
+            toks = slice(j * P, (j + 1) * P)
+            nc.vector.tensor_tensor(
+                out=uv_grouped[n][:, toks, :],
+                in0=u_sb[n][:, :, toks].rearrange("p t w -> p w t"),
+                in1=ht_ps[n, j][:].rearrange("p t w -> p w t"),
+                op=ALU.mult,
+            )
+
+        def quantise_uv(n, j):
+            if j == 0:
+                uv_codes[n] = work.tile([P, GROUP], U32, name="uv_codes", tag="uv_codes", align_bytes=64)
+                uv_scales[n] = work.tile([P, GROUP], U8, name="uv_scales", tag="uv_scales", align_bytes=64)
+            toks = slice(j * P, (j + 1) * P)
+            nc.vector.quantize_mx(
+                out=uv_codes[n][:, toks].bitcast(FP8X4),
+                scales=uv_scales[n][:, toks],
+                in_=uv_grouped[n][:, toks, :].rearrange("p w t -> p (w t)"),
+            )
+
+        def project_out(n, j):
+            o_ps[n, j] = psum.tile([P, WIDTH], F32, name="o", tag="o")
+            toks = slice(j * P, (j + 1) * P)
+            nc.tensor.matmul_mx(
+                out=o_ps[n, j][:],
+                lhsT=uv_codes[n][:, toks].bitcast(FP8X4),
+                lhsT_scale=uv_scales[n][:, toks],
+                rhs=wf_codes[:].bitcast(FP8X4),
+                rhs_scale=wf_scales[:],
+                start=True,
+                stop=True,
+            )
+
+        def add_bias(n, j):
+            if j == 0:
+                o_sb[n] = work.tile([P, TILES * WIDTH], F32, name="o_sb", tag="o_sb")
+            nc.vector.tensor_tensor(
+                out=o_sb[n][:, j * WIDTH : (j + 1) * WIDTH], in0=o_ps[n, j][:], in1=b_rows[:], op=ALU.add
+            )
+
+        def store(n):
+            nc.sync.dma_start(out=out_groups[n], in_=o_sb[n][:])
+
+        vec_rows = const.tile([P, P], BF16, name="vec_rows")
+        nc.vector.memset(vec_rows[:], 0.0)
+        nc.sync.dma_start(out=vec_rows[0:PACK, :], in_=bu.rearrange("(t p) -> t p", p=P))
+        nc.sync.dma_start(out=vec_rows[PACK : 2 * PACK, :], in_=g_norm.rearrange("(t p) -> t p", p=P))
+        b_row = const.tile([P, WIDTH], BF16, name="b_row")
+        nc.vector.memset(b_row[:], 0.0)
+        nc.sync.dma_start(out=b_row[0:1, :], in_=b_out.rearrange("(o c) -> o c", o=1))
+        wu_rows = const.tile([P, PACK * WIDTH], BF16, name="wu_rows")
+        nc.sync.dma_start(
+            out=wu_rows[:].rearrange("p (t c) -> p t c", t=PACK), in_=Wu.rearrange("(t p) c -> p t c", p=P)
+        )
+        load(0)
+        wf_rows = const.tile([P, PACK * WIDTH], BF16, name="wf_rows")
+        nc.sync.dma_start(
+            out=wf_rows[:].rearrange("p (t c) -> p t c", t=PACK), in_=Wf.rearrange("(t p) c -> p t c", p=P)
+        )
+
+        ident = const.tile([P, P], F32, name="ident")
+        make_identity(nc, ident[:])
+        ones = const.tile([P, P], BF16, name="ones")
+        nc.vector.memset(ones[:], 1.0)
+        minus_half = const.tile([P, TILES], F32, name="minus_half")
+        nc.vector.memset(minus_half[:], -0.5)
+
+        vec_f32 = const.tile([P, P], F32, name="vec_f32")
+        nc.vector.tensor_copy(out=vec_f32[:], in_=vec_rows[:])
+        vec_ps = psum.tile([P, PACK, P], F32, name="vec_ps", tag="ht")
+        nc.tensor.transpose(vec_ps[:, 0, :], vec_f32[:], ident[:])
+        bias_gain = const.tile([P, 2 * PACK], F32, name="bias_gain")
+        nc.vector.tensor_copy(out=bias_gain[:], in_=vec_ps[:, 0, 0 : 2 * PACK])
+
+        b_ps = psum.tile([P, WIDTH], F32, name="b_ps", tag="o")
+        nc.tensor.matmul(out=b_ps[:], lhsT=ones[:], rhs=b_row[:], start=True, stop=True)
+        b_rows = const.tile([P, WIDTH], F32, name="b_rows")
+        nc.vector.tensor_copy(out=b_rows[:], in_=b_ps[:])
+
+        wu_grouped = const.tile([P, WIDTH * PACK], BF16, name="wu_grouped", align_bytes=64)
+        wu_codes = const.tile([P, WIDTH], U32, name="wu_codes", align_bytes=64)
+        wu_scales = const.tile([P, WIDTH], U8, name="wu_scales", align_bytes=64)
+        for first in (0, 2):
+            regroup_word_pair(nc.vector.tensor_copy, transpose_word_pair(wu_rows, first), wu_grouped, first)
+        nc.vector.quantize_mx(out=wu_codes[:].bitcast(FP8X4), scales=wu_scales[:], in_=wu_grouped[:])
+
+        wf_f32 = const.tile([P, PACK * WIDTH], F32, name="wf_f32")
+        nc.vector.tensor_copy(out=wf_f32[:], in_=wf_rows[:])
+        wf_grouped = const.tile([P, WIDTH, PACK], BF16, name="wf_grouped", align_bytes=64)
+        wf_codes = const.tile([P, WIDTH], U32, name="wf_codes", align_bytes=64)
+        wf_scales = const.tile([P, WIDTH], U8, name="wf_scales", align_bytes=64)
+
+        def regroup_wf(c):
+            bank = transpose_f32_tile(wf_f32, c * WIDTH)
+            nc.vector.tensor_copy(out=wf_grouped[:, c * P : (c + 1) * P, :], in_=bank[:].rearrange("p t w -> p w t"))
+
+        def quantise_wf():
+            nc.vector.quantize_mx(
+                out=wf_codes[:].bitcast(FP8X4), scales=wf_scales[:], in_=wf_grouped[:].rearrange("p w t -> p (w t)")
+            )
+
+        for c in range(PACK):
+            regroup_wf(c)
+        quantise_wf()
+        for n in range(N_GROUPS):
+            if n > 0:
+                load(n)
+            for first in (0, 2):
+                transpose_x(n, first)
+                regroup_x(n, first)
+            quantise_x(n)
+            for j in range(TILES):
+                square_sum(n, j)
+            inverse_rms(n)
+            for j in range(TILES):
+                normalise(n, j)
+            for t in range(PACK):
+                project_up(n, t)
+                silu(n, t)
+                gain(n, t)
+            for j in range(TILES):
+                transpose_h(n, j)
+                multiply(n, j)
+                quantise_uv(n, j)
+                project_out(n, j)
+                add_bias(n, j)
+            store(n)

@@ -92,14 +92,12 @@ def tile_hstu_pb_t_kernel(tc, x, h_attn, Wu, bu, g_norm, Wf, b_out, out):
             if j == 0:
                 hn_sb[n] = work.tile([P, TILES * WIDTH], F32, name="hn_sb", tag="hn_sb")
             cols = slice(j * WIDTH, (j + 1) * WIDTH)
-            nc.gpsimd.tensor_scalar(
-                out=hn_sb[n][:, cols],
-                in0=h_sb[n][:, cols],
-                scalar1=rstd[n][:, j : j + 1],
-                scalar2=0.0,
-                op0=ALU.mult,
-                op1=ALU.add,
-            )
+            if j % 2 == 0:
+                nc.vector.tensor_scalar_mul(out=hn_sb[n][:, cols], in0=h_sb[n][:, cols], scalar1=rstd[n][:, j : j + 1])
+            else:
+                nc.scalar.activation(
+                    out=hn_sb[n][:, cols], in_=h_sb[n][:, cols], func=ACT.Copy, scale=rstd[n][:, j : j + 1]
+                )
 
         def transpose_x(n, first):
             xt_ps[n, first] = transpose_word_pair(x_sb[n], first)

@@ -30,8 +30,9 @@ def tile_hstu_pb_t_kernel(tc, x, h_attn, Wu, bu, g_norm, Wf, b_out, out):
     out_groups = out.flatten_outer_dims().rearrange("(n p j) c -> n p (j c)", p=P, j=TILES)
 
     with ExitStack() as ctx:
+        ctx.enter_context(tc.manual_schedule())
         const = ctx.enter_context(tc.tile_pool(name="const", bufs=1))
-        loads = ctx.enter_context(tc.tile_pool(name="loads", bufs=4))
+        loads = ctx.enter_context(tc.tile_pool(name="loads", bufs=5))
         work = ctx.enter_context(tc.tile_pool(name="work", bufs=3))
         psum = ctx.enter_context(tc.psum_pool(name="psum", bufs=2))
 
@@ -42,7 +43,7 @@ def tile_hstu_pb_t_kernel(tc, x, h_attn, Wu, bu, g_norm, Wf, b_out, out):
 
         def transpose_word_pair(rows, first):
             words = rows[:].bitcast(F32)
-            bank = psum.tile([P, 2, 2, P], F32, name="xt", tag="xt")
+            bank = psum.tile([P, 2, 2, P], F32, name="xt", tag="xt", bufs=1)
             for l in range(2):
                 for u in range(2):
                     col = (first + l) * (WIDTH // 2) + u * P
@@ -57,7 +58,7 @@ def tile_hstu_pb_t_kernel(tc, x, h_attn, Wu, bu, g_norm, Wf, b_out, out):
             )
 
         def transpose_f32_tile(rows, first_col):
-            bank = psum.tile([P, PACK, P], F32, name="ht", tag="ht")
+            bank = psum.tile([P, PACK, P], F32, name="ht", tag="ht", bufs=3)
             for t in range(PACK):
                 col = first_col + t * P
                 nc.tensor.transpose(bank[:, t, :], rows[:, col : col + P], ident[:])
@@ -92,12 +93,14 @@ def tile_hstu_pb_t_kernel(tc, x, h_attn, Wu, bu, g_norm, Wf, b_out, out):
             if j == 0:
                 hn_sb[n] = work.tile([P, TILES * WIDTH], F32, name="hn_sb", tag="hn_sb")
             cols = slice(j * WIDTH, (j + 1) * WIDTH)
-            if j % 2 == 0:
-                nc.vector.tensor_scalar_mul(out=hn_sb[n][:, cols], in0=h_sb[n][:, cols], scalar1=rstd[n][:, j : j + 1])
-            else:
-                nc.scalar.activation(
-                    out=hn_sb[n][:, cols], in_=h_sb[n][:, cols], func=ACT.Copy, scale=rstd[n][:, j : j + 1]
-                )
+            nc.gpsimd.tensor_scalar(
+                out=hn_sb[n][:, cols],
+                in0=h_sb[n][:, cols],
+                scalar1=rstd[n][:, j : j + 1],
+                scalar2=0.0,
+                op0=ALU.mult,
+                op1=ALU.add,
+            )
 
         def transpose_x(n, first):
             xt_ps[n, first] = transpose_word_pair(x_sb[n], first)
@@ -107,10 +110,16 @@ def tile_hstu_pb_t_kernel(tc, x, h_attn, Wu, bu, g_norm, Wf, b_out, out):
                 x_grouped[n] = work.tile([P, GROUP * PACK], BF16, name="x_grouped", tag="x_grouped", align_bytes=64)
             regroup_word_pair(nc.scalar.copy, xt_ps[n, first], x_grouped[n], first)
 
-        def quantise_x(n):
-            x_codes[n] = work.tile([P, GROUP], U32, name="x_codes", tag="x_codes", align_bytes=64)
-            x_scales[n] = work.tile([P, GROUP], U8, name="x_scales", tag="x_scales", align_bytes=64)
-            nc.vector.quantize_mx(out=x_codes[n][:].bitcast(FP8X4), scales=x_scales[n][:], in_=x_grouped[n][:])
+        def quantise_x(n, first):
+            if first == 0:
+                x_codes[n] = work.tile([P, GROUP], U32, name="x_codes", tag="x_codes", align_bytes=64)
+                x_scales[n] = work.tile([P, GROUP], U8, name="x_scales", tag="x_scales", align_bytes=64)
+            toks = slice(first * P, (first + 2) * P)
+            nc.vector.quantize_mx(
+                out=x_codes[n][:, toks].bitcast(FP8X4),
+                scales=x_scales[n][:, toks],
+                in_=x_grouped[n][:, first * P * PACK : (first + 2) * P * PACK],
+            )
 
         def project_up(n, t):
             z_ps[n, t] = psum.tile([P, GROUP], F32, name="z", tag="z")
@@ -182,8 +191,9 @@ def tile_hstu_pb_t_kernel(tc, x, h_attn, Wu, bu, g_norm, Wf, b_out, out):
                 out=o_sb[n][:, j * WIDTH : (j + 1) * WIDTH], in0=o_ps[n, j][:], in1=b_rows[:], op=ALU.add
             )
 
-        def store(n):
-            nc.sync.dma_start(out=out_groups[n], in_=o_sb[n][:])
+        def store(n, j):
+            cols = slice(j * WIDTH, (j + 1) * WIDTH)
+            nc.sync.dma_start(out=out_groups[n][:, cols], in_=o_sb[n][:, cols])
 
         vec_rows = const.tile([P, P], BF16, name="vec_rows")
         nc.vector.memset(vec_rows[:], 0.0)
@@ -204,17 +214,17 @@ def tile_hstu_pb_t_kernel(tc, x, h_attn, Wu, bu, g_norm, Wf, b_out, out):
 
         ident = const.tile([P, P], F32, name="ident")
         make_identity(nc, ident[:])
+        ident_bf16 = const.tile([P, P], BF16, name="ident_bf16")
+        make_identity(nc, ident_bf16[:])
         ones = const.tile([P, P], BF16, name="ones")
         nc.vector.memset(ones[:], 1.0)
         minus_half = const.tile([P, TILES], F32, name="minus_half")
         nc.vector.memset(minus_half[:], -0.5)
 
-        vec_f32 = const.tile([P, P], F32, name="vec_f32")
-        nc.vector.tensor_copy(out=vec_f32[:], in_=vec_rows[:])
-        vec_ps = psum.tile([P, PACK, P], F32, name="vec_ps", tag="ht")
-        nc.tensor.transpose(vec_ps[:, 0, :], vec_f32[:], ident[:])
+        vec_ps = psum.tile([P, P], BF16, name="vec_ps", tag="o")
+        nc.tensor.transpose(vec_ps[:], vec_rows[:], ident_bf16[:])
         bias_gain = const.tile([P, 2 * PACK], F32, name="bias_gain")
-        nc.vector.tensor_copy(out=bias_gain[:], in_=vec_ps[:, 0, 0 : 2 * PACK])
+        nc.vector.tensor_copy(out=bias_gain[:], in_=vec_ps[:, 0 : 2 * PACK])
 
         b_ps = psum.tile([P, WIDTH], F32, name="b_ps", tag="o")
         nc.tensor.matmul(out=b_ps[:], lhsT=ones[:], rhs=b_row[:], start=True, stop=True)
@@ -228,14 +238,15 @@ def tile_hstu_pb_t_kernel(tc, x, h_attn, Wu, bu, g_norm, Wf, b_out, out):
             regroup_word_pair(nc.vector.tensor_copy, transpose_word_pair(wu_rows, first), wu_grouped, first)
         nc.vector.quantize_mx(out=wu_codes[:].bitcast(FP8X4), scales=wu_scales[:], in_=wu_grouped[:])
 
-        wf_f32 = const.tile([P, PACK * WIDTH], F32, name="wf_f32")
-        nc.vector.tensor_copy(out=wf_f32[:], in_=wf_rows[:])
         wf_grouped = const.tile([P, WIDTH, PACK], BF16, name="wf_grouped", align_bytes=64)
         wf_codes = const.tile([P, WIDTH], U32, name="wf_codes", align_bytes=64)
         wf_scales = const.tile([P, WIDTH], U8, name="wf_scales", align_bytes=64)
 
         def regroup_wf(c):
-            bank = transpose_f32_tile(wf_f32, c * WIDTH)
+            bank = psum.tile([P, PACK, P], BF16, name="wf_ps", tag="o")
+            for t in range(PACK):
+                col = c * WIDTH + t * P
+                nc.tensor.transpose(bank[:, t, :], wf_rows[:, col : col + P], ident_bf16[:])
             nc.vector.tensor_copy(out=wf_grouped[:, c * P : (c + 1) * P, :], in_=bank[:].rearrange("p t w -> p w t"))
 
         def quantise_wf():
@@ -243,29 +254,39 @@ def tile_hstu_pb_t_kernel(tc, x, h_attn, Wu, bu, g_norm, Wf, b_out, out):
                 out=wf_codes[:].bitcast(FP8X4), scales=wf_scales[:], in_=wf_grouped[:].rearrange("p w t -> p (w t)")
             )
 
-        for c in range(PACK):
-            regroup_wf(c)
-        quantise_wf()
-        for n in range(N_GROUPS):
-            if n > 0:
-                load(n)
-            for first in (0, 2):
-                transpose_x(n, first)
-                regroup_x(n, first)
-            quantise_x(n)
-            for j in range(TILES):
-                square_sum(n, j)
-            inverse_rms(n)
-            for j in range(TILES):
-                normalise(n, j)
-            for t in range(PACK):
-                project_up(n, t)
-                silu(n, t)
-                gain(n, t)
-            for j in range(TILES):
-                transpose_h(n, j)
-                multiply(n, j)
-                quantise_uv(n, j)
-                project_out(n, j)
-                add_bias(n, j)
-            store(n)
+        def at(stage, tile_index):
+            n, j = divmod(tile_index, TILES)
+            if 0 <= n < N_GROUPS:
+                stage(n, j)
+
+        def at_pair(stage, tile_index):
+            if tile_index % 2 == 0:
+                at(stage, tile_index)
+
+        def at_group(stage, tile_index):
+            n, j = divmod(tile_index, TILES)
+            if j == 0 and 0 <= n < N_GROUPS:
+                stage(n)
+
+        for s in range(-3 * TILES, N_TILES + 3):
+            if s + 4 * TILES > 0:
+                at_group(load, s + 4 * TILES)
+            at(transpose_h, s + 2)
+            at_pair(transpose_x, s + 11)
+            at(project_up, s + 6)
+            at(project_out, s - 2)
+            at(square_sum, s + 7)
+            at_pair(regroup_x, s + 10)
+            at(silu, s + 5)
+            at_group(inverse_rms, s + 3)
+            at(normalise, s + 3)
+            at(multiply, s)
+            at(add_bias, s - 3)
+            at(gain, s + 4)
+            at(quantise_uv, s - 1)
+            at_pair(quantise_x, s + 9)
+            at(store, s - 3)
+            if -TILES <= s < 0:
+                regroup_wf(s + TILES)
+            if s == -1:
+                quantise_wf()

from contextlib import ExitStack

import concourse.mybir as mybir
from concourse.masks import make_identity

FP8X4 = mybir.dt.float8_e4m3fn_x4
BF16 = mybir.dt.bfloat16
F32 = mybir.dt.float32
U32 = mybir.dt.uint32
U8 = mybir.dt.uint8
ACT = mybir.ActivationFunctionType
ALU = mybir.AluOpType

P = 128
PACK = 4
WIDTH = P * PACK
TOKENS = 4 * 2048
TILES = 4
GROUP = TILES * P
N_GROUPS = TOKENS // GROUP
N_TILES = TOKENS // P
RMS_EPS = 1.1920928955078125e-07
FLOPS = 2 * 2 * TOKENS * WIDTH * WIDTH


def tile_hstu_pb_t_kernel(tc, x, h_attn, Wu, bu, g_norm, Wf, b_out, out):
    nc = tc.nc
    x_groups = x.flatten_outer_dims().rearrange("(n p j) c -> n p (j c)", p=P, j=TILES)
    h_groups = h_attn.flatten_outer_dims().rearrange("(n p j) c -> n p (j c)", p=P, j=TILES)
    out_groups = out.flatten_outer_dims().rearrange("(n p j) c -> n p (j c)", p=P, j=TILES)

    with ExitStack() as ctx:
        ctx.enter_context(tc.manual_schedule())
        const = ctx.enter_context(tc.tile_pool(name="const", bufs=1))
        loads = ctx.enter_context(tc.tile_pool(name="loads", bufs=5))
        work = ctx.enter_context(tc.tile_pool(name="work", bufs=3))
        psum = ctx.enter_context(tc.psum_pool(name="psum", bufs=2))

        x_sb, h_sb, hn_sb, sumsq, rstd = {}, {}, {}, {}, {}
        x_grouped, x_codes, x_scales = {}, {}, {}
        u_sb, uv_grouped, uv_codes, uv_scales, o_sb = {}, {}, {}, {}, {}
        xt_ps, z_ps, ht_ps, o_ps = {}, {}, {}, {}

        def transpose_word_pair(rows, first):
            words = rows[:].bitcast(F32)
            bank = psum.tile([P, 2, 2, P], F32, name="xt", tag="xt", bufs=1)
            for l in range(2):
                for u in range(2):
                    col = (first + l) * (WIDTH // 2) + u * P
                    nc.tensor.transpose(bank[:, l, u, :], words[:, col : col + P], ident[:])
            return bank

        def regroup_word_pair(copy, bank, grouped, first):
            words = grouped[:].bitcast(F32)[:, first * 2 * P : (first + 2) * 2 * P]
            copy(
                out=words.rearrange("p (l w u) -> p l w u", l=2, u=2),
                in_=bank[:].rearrange("p l u w -> p l w u"),
            )

        def transpose_f32_tile(rows, first_col):
            bank = psum.tile([P, PACK, P], F32, name="ht", tag="ht", bufs=3)
            for t in range(PACK):
                col = first_col + t * P
                nc.tensor.transpose(bank[:, t, :], rows[:, col : col + P], ident[:])
            return bank

        def load(n):
            x_sb[n] = loads.tile([P, TILES * WIDTH], BF16, name="x_sb", tag="x_sb")
            nc.sync.dma_start(out=x_sb[n][:], in_=x_groups[n])
            h_sb[n] = loads.tile([P, TILES * WIDTH], BF16, name="h_sb", tag="h_sb")
            nc.sync.dma_start(out=h_sb[n][:], in_=h_groups[n])

        def square_sum(n, j):
            if j == 0:
                sumsq[n] = work.tile([P, TILES], F32, name="sumsq", tag="sumsq")
            squares = work.tile([P, WIDTH], BF16, name="squares", tag="squares")
            nc.scalar.activation(
                out=squares[:],
                in_=h_sb[n][:, j * WIDTH : (j + 1) * WIDTH],
                func=ACT.Square,
                accum_out=sumsq[n][:, j : j + 1],
            )

        def inverse_rms(n):
            mean = work.tile([P, TILES], F32, name="mean", tag="mean")
            nc.gpsimd.tensor_scalar(
                out=mean[:], in0=sumsq[n][:], scalar1=1.0 / WIDTH, scalar2=RMS_EPS, op0=ALU.mult, op1=ALU.add
            )
            rstd[n] = work.tile([P, TILES], F32, name="rstd", tag="rstd")
            nc.gpsimd.tensor_tensor(out=rstd[n][:], in0=mean[:], in1=minus_half[:], op=ALU.pow)

        def normalise(n, j):
            if j == 0:
                hn_sb[n] = work.tile([P, TILES * WIDTH], F32, name="hn_sb", tag="hn_sb")
            cols = slice(j * WIDTH, (j + 1) * WIDTH)
            nc.gpsimd.tensor_scalar(
                out=hn_sb[n][:, cols],
                in0=h_sb[n][:, cols],
                scalar1=rstd[n][:, j : j + 1],
                scalar2=0.0,
                op0=ALU.mult,
                op1=ALU.add,
            )

        def transpose_x(n, first):
            xt_ps[n, first] = transpose_word_pair(x_sb[n], first)

        def regroup_x(n, first):
            if first == 0:
                x_grouped[n] = work.tile([P, GROUP * PACK], BF16, name="x_grouped", tag="x_grouped", align_bytes=64)
            regroup_word_pair(nc.scalar.copy, xt_ps[n, first], x_grouped[n], first)

        def quantise_x(n, first):
            if first == 0:
                x_codes[n] = work.tile([P, GROUP], U32, name="x_codes", tag="x_codes", align_bytes=64)
                x_scales[n] = work.tile([P, GROUP], U8, name="x_scales", tag="x_scales", align_bytes=64)
            toks = slice(first * P, (first + 2) * P)
            nc.vector.quantize_mx(
                out=x_codes[n][:, toks].bitcast(FP8X4),
                scales=x_scales[n][:, toks],
                in_=x_grouped[n][:, first * P * PACK : (first + 2) * P * PACK],
            )

        def project_up(n, t):
            z_ps[n, t] = psum.tile([P, GROUP], F32, name="z", tag="z")
            cols = slice(t * P, (t + 1) * P)
            nc.tensor.matmul_mx(
                out=z_ps[n, t][:],
                lhsT=wu_codes[:, cols].bitcast(FP8X4),
                lhsT_scale=wu_scales[:, cols],
                rhs=x_codes[n][:].bitcast(FP8X4),
                rhs_scale=x_scales[n][:],
                start=True,
                stop=True,
            )

        def silu(n, t):
            if t == 0:
                u_sb[n] = work.tile([P, PACK, GROUP], F32, name="u_sb", tag="u_sb")
            nc.scalar.activation(
                out=u_sb[n][:, t, :], in_=z_ps[n, t][:], func=ACT.Silu, bias=bias_gain[:, t : t + 1], scale=1.0
            )

        def gain(n, t):
            nc.vector.tensor_scalar_mul(
                out=u_sb[n][:, t, :], in0=u_sb[n][:, t, :], scalar1=bias_gain[:, PACK + t : PACK + t + 1]
            )

        def transpose_h(n, j):
            ht_ps[n, j] = transpose_f32_tile(hn_sb[n], j * WIDTH)

        def multiply(n, j):
            if j == 0:
                uv_grouped[n] = work.tile([P, GROUP, PACK], BF16, name="uv_grouped", tag="uv_grouped", align_bytes=64)
            toks = slice(j * P, (j + 1) * P)
            nc.vector.tensor_tensor(
                out=uv_grouped[n][:, toks, :],
                in0=u_sb[n][:, :, toks].rearrange("p t w -> p w t"),
                in1=ht_ps[n, j][:].rearrange("p t w -> p w t"),
                op=ALU.mult,
            )

        def quantise_uv(n, j):
            if j == 0:
                uv_codes[n] = work.tile([P, GROUP], U32, name="uv_codes", tag="uv_codes", align_bytes=64)
                uv_scales[n] = work.tile([P, GROUP], U8, name="uv_scales", tag="uv_scales", align_bytes=64)
            toks = slice(j * P, (j + 1) * P)
            nc.vector.quantize_mx(
                out=uv_codes[n][:, toks].bitcast(FP8X4),
                scales=uv_scales[n][:, toks],
                in_=uv_grouped[n][:, toks, :].rearrange("p w t -> p (w t)"),
            )

        def project_out(n, j):
            o_ps[n, j] = psum.tile([P, WIDTH], F32, name="o", tag="o")
            toks = slice(j * P, (j + 1) * P)
            nc.tensor.matmul_mx(
                out=o_ps[n, j][:],
                lhsT=uv_codes[n][:, toks].bitcast(FP8X4),
                lhsT_scale=uv_scales[n][:, toks],
                rhs=wf_codes[:].bitcast(FP8X4),
                rhs_scale=wf_scales[:],
                start=True,
                stop=True,
            )

        def add_bias(n, j):
            if j == 0:
                o_sb[n] = work.tile([P, TILES * WIDTH], F32, name="o_sb", tag="o_sb")
            nc.vector.tensor_tensor(
                out=o_sb[n][:, j * WIDTH : (j + 1) * WIDTH], in0=o_ps[n, j][:], in1=b_rows[:], op=ALU.add
            )

        def store(n, j):
            cols = slice(j * WIDTH, (j + 1) * WIDTH)
            nc.sync.dma_start(out=out_groups[n][:, cols], in_=o_sb[n][:, cols])

        vec_rows = const.tile([P, P], BF16, name="vec_rows")
        nc.vector.memset(vec_rows[:], 0.0)
        nc.sync.dma_start(out=vec_rows[0:PACK, :], in_=bu.rearrange("(t p) -> t p", p=P))
        nc.sync.dma_start(out=vec_rows[PACK : 2 * PACK, :], in_=g_norm.rearrange("(t p) -> t p", p=P))
        b_row = const.tile([P, WIDTH], BF16, name="b_row")
        nc.vector.memset(b_row[:], 0.0)
        nc.sync.dma_start(out=b_row[0:1, :], in_=b_out.rearrange("(o c) -> o c", o=1))
        wu_rows = const.tile([P, PACK * WIDTH], BF16, name="wu_rows")
        nc.sync.dma_start(
            out=wu_rows[:].rearrange("p (t c) -> p t c", t=PACK), in_=Wu.rearrange("(t p) c -> p t c", p=P)
        )
        load(0)
        wf_rows = const.tile([P, PACK * WIDTH], BF16, name="wf_rows")
        nc.sync.dma_start(
            out=wf_rows[:].rearrange("p (t c) -> p t c", t=PACK), in_=Wf.rearrange("(t p) c -> p t c", p=P)
        )

        ident = const.tile([P, P], F32, name="ident")
        make_identity(nc, ident[:])
        ident_bf16 = const.tile([P, P], BF16, name="ident_bf16")
        make_identity(nc, ident_bf16[:])
        ones = const.tile([P, P], BF16, name="ones")
        nc.vector.memset(ones[:], 1.0)
        minus_half = const.tile([P, TILES], F32, name="minus_half")
        nc.vector.memset(minus_half[:], -0.5)

        vec_ps = psum.tile([P, P], BF16, name="vec_ps", tag="o")
        nc.tensor.transpose(vec_ps[:], vec_rows[:], ident_bf16[:])
        bias_gain = const.tile([P, 2 * PACK], F32, name="bias_gain")
        nc.vector.tensor_copy(out=bias_gain[:], in_=vec_ps[:, 0 : 2 * PACK])

        b_ps = psum.tile([P, WIDTH], F32, name="b_ps", tag="o")
        nc.tensor.matmul(out=b_ps[:], lhsT=ones[:], rhs=b_row[:], start=True, stop=True)
        b_rows = const.tile([P, WIDTH], F32, name="b_rows")
        nc.vector.tensor_copy(out=b_rows[:], in_=b_ps[:])

        wu_grouped = const.tile([P, WIDTH * PACK], BF16, name="wu_grouped", align_bytes=64)
        wu_codes = const.tile([P, WIDTH], U32, name="wu_codes", align_bytes=64)
        wu_scales = const.tile([P, WIDTH], U8, name="wu_scales", align_bytes=64)
        for first in (0, 2):
            regroup_word_pair(nc.vector.tensor_copy, transpose_word_pair(wu_rows, first), wu_grouped, first)
        nc.vector.quantize_mx(out=wu_codes[:].bitcast(FP8X4), scales=wu_scales[:], in_=wu_grouped[:])

        wf_grouped = const.tile([P, WIDTH, PACK], BF16, name="wf_grouped", align_bytes=64)
        wf_codes = const.tile([P, WIDTH], U32, name="wf_codes", align_bytes=64)
        wf_scales = const.tile([P, WIDTH], U8, name="wf_scales", align_bytes=64)

        def regroup_wf(c):
            bank = psum.tile([P, PACK, P], BF16, name="wf_ps", tag="o")
            for t in range(PACK):
                col = c * WIDTH + t * P
                nc.tensor.transpose(bank[:, t, :], wf_rows[:, col : col + P], ident_bf16[:])
            nc.vector.tensor_copy(out=wf_grouped[:, c * P : (c + 1) * P, :], in_=bank[:].rearrange("p t w -> p w t"))

        def quantise_wf():
            nc.vector.quantize_mx(
                out=wf_codes[:].bitcast(FP8X4), scales=wf_scales[:], in_=wf_grouped[:].rearrange("p w t -> p (w t)")
            )

        def at(stage, tile_index):
            n, j = divmod(tile_index, TILES)
            if 0 <= n < N_GROUPS:
                stage(n, j)

        def at_pair(stage, tile_index):
            if tile_index % 2 == 0:
                at(stage, tile_index)

        def at_group(stage, tile_index):
            n, j = divmod(tile_index, TILES)
            if j == 0 and 0 <= n < N_GROUPS:
                stage(n)

        for s in range(-3 * TILES, N_TILES + 3):
            if s + 4 * TILES > 0:
                at_group(load, s + 4 * TILES)
            at(transpose_h, s + 2)
            at_pair(transpose_x, s + 11)
            at(project_up, s + 6)
            at(project_out, s - 2)
            at(square_sum, s + 7)
            at_pair(regroup_x, s + 10)
            at(silu, s + 5)
            at_group(inverse_rms, s + 3)
            at(normalise, s + 3)
            at(multiply, s)
            at(add_bias, s - 3)
            at(gain, s + 4)
            at(quantise_uv, s - 1)
            at_pair(quantise_x, s + 9)
            at(store, s - 3)
            if -TILES <= s < 0:
                regroup_wf(s + TILES)
            if s == -1:
                quantise_wf()
